import numpy as np
import ml_dtypes


def mxq(x, axis, fmt="e4m3"):
    dtype, down = {"e4m3": (ml_dtypes.float8_e4m3fn, 7), "e5m2": (ml_dtypes.float8_e5m2, 14)}[fmt]
    v = np.moveaxis(np.asarray(x, np.float32).astype(ml_dtypes.bfloat16).astype(np.float64), axis, -1)
    blocks = v.reshape(v.shape[:-1] + (-1, 32))
    amax = np.abs(blocks).max(-1, keepdims=True)
    byte = np.maximum(np.where(amax > 0, np.frexp(amax)[1] - 1 + 127, 0) - down, 1)
    scale = np.exp2(byte - 127.0)
    codes = (blocks / scale).astype(np.float32).astype(dtype).astype(np.float64)
    return np.moveaxis((codes * scale).reshape(v.shape), -1, axis)


WIDE = False


def mx_kscale(k):
    if not WIDE:
        return np.ones(k)
    levels = np.array([10, -10, 5, -5, 0])
    a = np.random.permutation(np.resize(levels, k // 512 * 4)).reshape(k // 512, 4)
    idx = np.arange(k)
    return np.exp2(a[idx // 512, idx % 128 // 32])


BF16 = ml_dtypes.bfloat16


def bf(x):
    return np.asarray(x, np.float32).astype(BF16)


def f64(x):
    return np.asarray(x).astype(np.float64)


B, C, D, DV, H, W = 1, 1024, 128, 512, 64, 32
N = H * W
M = (H // 2) * (W // 2)


def setup_inputs():
    t = mx_kscale(DV)
    return {"q": bf(np.random.standard_normal((B, N, D)) * 0.5),
            "k": bf((1.0 + 0.7 * np.random.standard_normal((B, D, M))) * 0.5),
            "v": bf((1.0 + 0.7 * np.random.standard_normal((B, DV, M))) * t[None, :, None]),
            "Wo": bf(np.random.standard_normal((C, DV)) / np.sqrt(DV) / t[None, :]),
            "gamma": bf(1.0 + 0.1 * np.random.standard_normal(1)),
            "x": bf(np.random.standard_normal((B, C, H, W)))}


def reference(q, k, v, Wo, gamma, x):
    s = f64(q) @ f64(k)
    e = np.exp(s - s.max(-1, keepdims=True))
    o = (mxq(f64(v), 2, "e4m3") @ mxq(e, 2, "e4m3").transpose(0, 2, 1)) / e.sum(-1)[:, None, :]
    y = mxq(f64(Wo), 1, "e4m3") @ mxq(o, 1, "e4m3")
    return (f64(gamma)[0] * y).reshape(B, C, H, W) + f64(x)

@@ -1,0 +1,270 @@
+from contextlib import ExitStack
+
+import concourse.mybir as mybir
+from concourse.masks import make_identity
+
+F32 = mybir.dt.float32
+BF16 = mybir.dt.bfloat16
+U32 = mybir.dt.uint32
+U8 = mybir.dt.uint8
+FP8X4 = mybir.dt.float8_e4m3fn_x4
+ACT = mybir.ActivationFunctionType
+ALU = mybir.AluOpType
+
+P = 128
+N_POS = 2048
+D_QK = 128
+K_MX = 512
+C_OUT = 1024
+HALVES = 2
+PACK = 4
+
+N_TILES = N_POS // P
+C_TILES = C_OUT // P
+V_TILES = K_MX // P
+GROUP = 4
+N_GROUPS = N_TILES // GROUP
+PAIR = 2
+V_PAIRS = V_TILES // PAIR
+WO_PAIRS = C_TILES // PAIR
+Y_BANKS = 2
+C_PER_BANK = C_TILES // Y_BANKS
+
+FLOPS = 2 * N_POS * (D_QK * K_MX + K_MX * K_MX + C_OUT * K_MX)
+
+
+def tile_selfattention_pb_kernel(tc, q, k, v, Wo, gamma, x, out):
+    nc = tc.nc
+
+    q_view = q.rearrange("b (a p) d -> p (b a) d", p=P)
+    k_view = k.rearrange("b d m -> d (b m)")
+    v_view = v.rearrange("b (t p) m -> p (b t) m", p=P)
+    wo_view = Wo.rearrange("(t p) c -> p t c", p=P)
+    x_view = x.rearrange("b (t p) h w -> p (b t) (h w)", p=P)
+    out_view = out.rearrange("b (t p) h w -> p (b t) (h w)", p=P)
+
+    with ExitStack() as ctx:
+        keep = ctx.enter_context(tc.tile_pool(name="keep", bufs=1))
+        work = ctx.enter_context(tc.tile_pool(name="work", bufs=3))
+        psum = ctx.enter_context(tc.psum_pool(name="psum", bufs=1))
+        ctx.enter_context(tc.manual_schedule())
+
+        ident_bf16 = keep.tile([P, P], BF16, name="ident_bf16")
+        ident_f32 = keep.tile([P, P], F32, name="ident_f32")
+        q_rows = keep.tile([P, N_TILES, D_QK], BF16, name="q_rows")
+        q_flipped = keep.tile([P, N_POS], BF16, name="q_flipped")
+        k_sb = keep.tile([P, K_MX], BF16, name="k_sb")
+        v_rows = keep.tile([P, V_TILES, K_MX], BF16, name="v_rows")
+        wo_rows = keep.tile([P, C_TILES, K_MX], BF16, name="wo_rows")
+        x_sb = keep.tile([P, N_GROUPS, C_TILES, GROUP * P], BF16, name="x_sb")
+        gamma_bf16 = keep.tile([P, 1], BF16, name="gamma_bf16")
+        gamma_f32 = keep.tile([P, 1], F32, name="gamma_f32")
+        v_codes = keep.tile([P, K_MX], U32, name="v_codes", align_bytes=64)
+        v_scales = keep.tile([P, K_MX], U8, name="v_scales", align_bytes=64)
+        wo_codes = keep.tile([P, C_OUT], U32, name="wo_codes", align_bytes=64)
+        wo_scales = keep.tile([P, C_OUT], U8, name="wo_scales", align_bytes=64)
+        neg_max = keep.tile([P, N_TILES], F32, name="neg_max")
+        row_sum = keep.tile([P, N_TILES], F32, name="row_sum")
+        inv_sum = keep.tile([P, N_TILES], F32, name="inv_sum")
+
+        make_identity(nc, ident_bf16[:])
+        make_identity(nc, ident_f32[:])
+
+        def load_q(g):
+            tiles = slice(g * GROUP, (g + 1) * GROUP)
+            nc.sync.dma_start(out=q_rows[:, tiles, :], in_=q_view[:, tiles, :])
+
+        def load_pair(rows, view, b):
+            tiles = slice(b * PAIR, (b + 1) * PAIR)
+            nc.sync.dma_start(out=rows[:, tiles, :], in_=view[:, tiles, :])
+
+        nc.scalar.dma_start(out=gamma_bf16[:], in_=gamma.partition_broadcast(P))
+        load_q(0)
+        nc.sync.dma_start(out=k_sb[:], in_=k_view)
+        for b in range(V_PAIRS):
+            load_pair(v_rows, v_view, b)
+        load_q(1)
+        for b in range(WO_PAIRS):
+            load_pair(wo_rows, wo_view, b)
+        load_q(2)
+        load_q(3)
+        for g in range(N_GROUPS):
+            nc.sync.dma_start(
+                out=x_sb[:, g, :, :], in_=x_view[:, :, g * GROUP * P : (g + 1) * GROUP * P]
+            )
+        nc.vector.tensor_copy(out=gamma_f32[:], in_=gamma_bf16[:])
+
+        def flip(row_tiles):
+            bank = psum.tile([P, len(row_tiles), HALVES, P], F32, name="flip_bank", tag="flip", bufs=3)
+            for a, rows in enumerate(row_tiles):
+                words = rows.bitcast(F32)
+                for u in range(HALVES):
+                    nc.tensor.transpose(
+                        out=bank[:, a, u, :], in_=words[:, u * P : (u + 1) * P], identity=ident_f32[:]
+                    )
+            return bank
+
+        def regroup(copy, bank, name):
+            tiles = bank.shape[1]
+            grouped = work.tile([P, tiles * P * PACK], BF16, name=name, tag=name, align_bytes=64)
+            copy(
+                out=grouped[:].bitcast(F32).rearrange("p (a r u) -> p a r u", a=tiles, u=HALVES),
+                in_=bank[:].rearrange("p a u r -> p a r u"),
+            )
+            return grouped
+
+        def quantise(grouped, codes, scales):
+            nc.vector.quantize_mx(out=codes.bitcast(FP8X4), scales=scales, in_=grouped[:])
+
+        live = {}
+
+        def flip_v(b):
+            bank = flip([v_rows[:, b * PAIR + a, :] for a in range(PAIR)])
+            live["v_grouped", b] = regroup(nc.scalar.copy, bank, "v_grouped")
+
+        def quantise_v(b):
+            cols = slice(b * PAIR * P, (b + 1) * PAIR * P)
+            quantise(live["v_grouped", b], v_codes[:, cols], v_scales[:, cols])
+
+        def flip_wo(b):
+            live["wo_bank", b] = flip([wo_rows[:, b * PAIR + a, :] for a in range(PAIR)])
+
+        def regroup_wo(b):
+            live["wo_grouped", b] = regroup(nc.vector.tensor_copy, live["wo_bank", b], "wo_grouped")
+
+        def quantise_wo(b):
+            cols = slice(b * PAIR * P, (b + 1) * PAIR * P)
+            quantise(live["wo_grouped", b], wo_codes[:, cols], wo_scales[:, cols])
+
+        def flip_q(g):
+            bank = psum.tile([P, GROUP, P], BF16, name="q_bank", tag="flip", bufs=3)
+            for a in range(GROUP):
+                nc.tensor.transpose(
+                    out=bank[:, a, :], in_=q_rows[:, g * GROUP + a, :], identity=ident_bf16[:]
+                )
+            nc.scalar.copy(
+                out=q_flipped[:, g * GROUP * P : (g + 1) * GROUP * P],
+                in_=bank[:].rearrange("p a r -> p (a r)"),
+            )
+
+        def scores(i):
+            s_bank = psum.tile([P, K_MX], F32, name="s_bank", tag="scores", bufs=2)
+            nc.tensor.matmul(
+                out=s_bank[:], lhsT=q_flipped[:, i * P : (i + 1) * P], rhs=k_sb[:], start=True, stop=True
+            )
+            live["s", i] = s_bank
+
+        def row_maximum(i):
+            nc.vector.tensor_reduce(
+                out=neg_max[:, i : i + 1],
+                in_=live["s", i][:],
+                axis=mybir.AxisListType.X,
+                op=ALU.max,
+                negate=True,
+            )
+
+        def exponentials(i):
+            e_rows = work.tile([P, K_MX], BF16, name="e_rows")
+            nc.scalar.activation(
+                out=e_rows[:],
+                in_=live["s", i][:],
+                func=ACT.Exp,
+                bias=neg_max[:, i : i + 1],
+                scale=1.0,
+                accum_out=row_sum[:, i : i + 1],
+            )
+            live["e_rows", i] = e_rows
+
+        def flip_e(i):
+            live["e_grouped", i] = regroup(nc.scalar.copy, flip([live["e_rows", i][:]]), "e_grouped")
+
+        def quantise_e(i):
+            e_codes = work.tile([P, P], U32, name="e_codes", align_bytes=64)
+            e_scales = work.tile([P, P], U8, name="e_scales", align_bytes=64)
+            quantise(live["e_grouped", i], e_codes[:], e_scales[:])
+            live["e_codes", i] = e_codes
+            live["e_scales", i] = e_scales
+            nc.vector.reciprocal(out=inv_sum[:, i : i + 1], in_=row_sum[:, i : i + 1])
+
+        def attend(i):
+            attn_bank = psum.tile([P, K_MX], F32, name="attn_bank", tag="attn", bufs=1)
+            nc.tensor.matmul_mx(
+                out=attn_bank[:],
+                lhsT=live["e_codes", i][:].bitcast(FP8X4),
+                lhsT_scale=live["e_scales", i][:],
+                rhs=v_codes[:].bitcast(FP8X4),
+                rhs_scale=v_scales[:],
+                start=True,
+                stop=True,
+            )
+            o_rows = work.tile([P, K_MX], BF16, name="o_rows")
+            nc.scalar.activation(
+                out=o_rows[:], in_=attn_bank[:], func=ACT.Copy, scale=inv_sum[:, i : i + 1]
+            )
+            live["o_rows", i] = o_rows
+
+        def flip_o(i):
+            live["o_grouped", i] = regroup(nc.scalar.copy, flip([live["o_rows", i][:]]), "o_grouped")
+
+        def quantise_o(i):
+            o_codes = work.tile([P, P], U32, name="o_codes", align_bytes=64)
+            o_scales = work.tile([P, P], U8, name="o_scales", align_bytes=64)
+            quantise(live["o_grouped", i], o_codes[:], o_scales[:])
+            live["o_codes", i] = o_codes
+            live["o_scales", i] = o_scales
+
+        def project(i):
+            for h in range(Y_BANKS):
+                y_bank = psum.tile([P, C_PER_BANK, P], F32, name="y_bank", tag="proj", bufs=2)
+                for j in range(C_PER_BANK):
+                    cols = slice((h * C_PER_BANK + j) * P, (h * C_PER_BANK + j + 1) * P)
+                    nc.tensor.matmul_mx(
+                        out=y_bank[:, j, :],
+                        lhsT=wo_codes[:, cols].bitcast(FP8X4),
+                        lhsT_scale=wo_scales[:, cols],
+                        rhs=live["o_codes", i][:].bitcast(FP8X4),
+                        rhs_scale=live["o_scales", i][:],
+                        start=True,
+                        stop=True,
+                    )
+                live["y", i, h] = y_bank
+
+        def finish(i):
+            a = i % GROUP
+            for h in range(Y_BANKS):
+                c_tiles = slice(h * C_PER_BANK, (h + 1) * C_PER_BANK)
+                result = work.tile([P, C_PER_BANK, P], F32, name="result", bufs=6)
+                nc.vector.scalar_tensor_tensor(
+                    out=result[:],
+                    in0=live["y", i, h][:],
+                    scalar=gamma_f32[:, 0:1],
+                    in1=x_sb[:, i // GROUP, c_tiles, a * P : (a + 1) * P],
+                    op0=ALU.mult,
+                    op1=ALU.add,
+                )
+                nc.sync.dma_start(out=out_view[:, c_tiles, i * P : (i + 1) * P], in_=result[:])
+
+        def stage(step, i, count):
+            if 0 <= i < count:
+                step(i)
+
+        flip_q(0)
+        scores(0)
+        for c in range(N_TILES + 6):
+            stage(project, c - 6, N_TILES)
+            stage(row_maximum, c, N_TILES)
+            stage(regroup_wo, c - 2, WO_PAIRS)
+            stage(finish, c - 6, N_TILES)
+            stage(exponentials, c, N_TILES)
+            stage(attend, c - 3, N_TILES)
+            stage(flip_e, c - 1, N_TILES)
+            stage(flip_o, c - 4, N_TILES)
+            stage(scores, c + 1, N_TILES)
+            stage(flip_v, c, V_PAIRS)
+            stage(flip_wo, c - 1, WO_PAIRS)
+            if c % GROUP == 1:
+                stage(flip_q, c // GROUP + 1, N_GROUPS)
+            stage(quantise_e, c - 2, N_TILES)
+            stage(quantise_o, c - 5, N_TILES)
+            stage(quantise_v, c - 1, V_PAIRS)
+            stage(quantise_wo, c - 2, WO_PAIRS)

@@ -254,6 +254,8 @@ def tile_selfattention_pb_kernel(tc, q, k, v, Wo, gamma, x, out):
             stage(project, c - 6, N_TILES)
             stage(row_maximum, c, N_TILES)
             stage(regroup_wo, c - 2, WO_PAIRS)
+            stage(quantise_e, c - 2, N_TILES)
+            stage(quantise_o, c - 5, N_TILES)
             stage(finish, c - 6, N_TILES)
             stage(exponentials, c, N_TILES)
             stage(attend, c - 3, N_TILES)
@@ -264,7 +266,5 @@ def tile_selfattention_pb_kernel(tc, q, k, v, Wo, gamma, x, out):
             stage(flip_wo, c - 1, WO_PAIRS)
             if c % GROUP == 1:
                 stage(flip_q, c // GROUP + 1, N_GROUPS)
-            stage(quantise_e, c - 2, N_TILES)
-            stage(quantise_o, c - 5, N_TILES)
             stage(quantise_v, c - 1, V_PAIRS)
             stage(quantise_wo, c - 2, WO_PAIRS)

@@ -47,7 +47,6 @@ def tile_selfattention_pb_kernel(tc, q, k, v, Wo, gamma, x, out):
         keep = ctx.enter_context(tc.tile_pool(name="keep", bufs=1))
         work = ctx.enter_context(tc.tile_pool(name="work", bufs=3))
         psum = ctx.enter_context(tc.psum_pool(name="psum", bufs=1))
-        ctx.enter_context(tc.manual_schedule())
 
         ident_bf16 = keep.tile([P, P], BF16, name="ident_bf16")
         ident_f32 = keep.tile([P, P], F32, name="ident_f32")

@@ -24,6 +24,8 @@ C_TILES = C_OUT // P
 V_TILES = K_MX // P
 GROUP = 4
 N_GROUPS = N_TILES // GROUP
+N_HALVES = 2
+N_HALF = N_POS // N_HALVES
 PAIR = 2
 V_PAIRS = V_TILES // PAIR
 WO_PAIRS = C_TILES // PAIR
@@ -38,8 +40,8 @@ def tile_selfattention_pb_kernel(tc, q, k, v, Wo, gamma, x, out):
 
     q_view = q.rearrange("b (a p) d -> p (b a) d", p=P)
     k_view = k.rearrange("b d m -> d (b m)")
-    v_view = v.rearrange("b (t p) m -> p (b t) m", p=P)
-    wo_view = Wo.rearrange("(t p) c -> p t c", p=P)
+    v_view = v.rearrange("b (t p a) m -> p (b t) a m", p=P, a=PAIR)
+    wo_view = Wo.rearrange("(t p a) c -> p t a c", p=P, a=PAIR)
     x_view = x.rearrange("b (t p) h w -> p (b t) (h w)", p=P)
     out_view = out.rearrange("b (t p) h w -> p (b t) (h w)", p=P)
 
@@ -53,9 +55,9 @@ def tile_selfattention_pb_kernel(tc, q, k, v, Wo, gamma, x, out):
         q_rows = keep.tile([P, N_TILES, D_QK], BF16, name="q_rows")
         q_flipped = keep.tile([P, N_POS], BF16, name="q_flipped")
         k_sb = keep.tile([P, K_MX], BF16, name="k_sb")
-        v_rows = keep.tile([P, V_TILES, K_MX], BF16, name="v_rows")
-        wo_rows = keep.tile([P, C_TILES, K_MX], BF16, name="wo_rows")
-        x_sb = keep.tile([P, N_GROUPS, C_TILES, GROUP * P], BF16, name="x_sb")
+        v_rows = keep.tile([P, V_PAIRS, PAIR, K_MX], BF16, name="v_rows")
+        wo_rows = keep.tile([P, WO_PAIRS, PAIR, K_MX], BF16, name="wo_rows")
+        x_sb = keep.tile([P, N_HALVES, C_TILES, N_HALF], BF16, name="x_sb")
         gamma_bf16 = keep.tile([P, 1], BF16, name="gamma_bf16")
         gamma_f32 = keep.tile([P, 1], F32, name="gamma_f32")
         v_codes = keep.tile([P, K_MX], U32, name="v_codes", align_bytes=64)
@@ -66,6 +68,10 @@ def tile_selfattention_pb_kernel(tc, q, k, v, Wo, gamma, x, out):
         row_sum = keep.tile([P, N_TILES], F32, name="row_sum")
         inv_sum = keep.tile([P, N_TILES], F32, name="inv_sum")
 
+        warm_in = keep.tile([P, 1], F32, name="warm_in")
+        warm_out = keep.tile([P, 1], F32, name="warm_out")
+        nc.vector.memset(warm_in[:], 0.0)
+        nc.scalar.activation(out=warm_out[:], in_=warm_in[:], func=ACT.Exp)
         make_identity(nc, ident_bf16[:])
         make_identity(nc, ident_f32[:])
 
@@ -74,8 +80,7 @@ def tile_selfattention_pb_kernel(tc, q, k, v, Wo, gamma, x, out):
             nc.sync.dma_start(out=q_rows[:, tiles, :], in_=q_view[:, tiles, :])
 
         def load_pair(rows, view, b):
-            tiles = slice(b * PAIR, (b + 1) * PAIR)
-            nc.sync.dma_start(out=rows[:, tiles, :], in_=view[:, tiles, :])
+            nc.sync.dma_start(out=rows[:, b, :, :], in_=view[:, b, :, :])
 
         nc.scalar.dma_start(out=gamma_bf16[:], in_=gamma.partition_broadcast(P))
         load_q(0)
@@ -87,10 +92,12 @@ def tile_selfattention_pb_kernel(tc, q, k, v, Wo, gamma, x, out):
             load_pair(wo_rows, wo_view, b)
         load_q(2)
         load_q(3)
-        for g in range(N_GROUPS):
-            nc.sync.dma_start(
-                out=x_sb[:, g, :, :], in_=x_view[:, :, g * GROUP * P : (g + 1) * GROUP * P]
-            )
+        for g in range(N_HALVES):
+            for h in range(Y_BANKS):
+                c_tiles = slice(h * C_PER_BANK, (h + 1) * C_PER_BANK)
+                nc.sync.dma_start(
+                    out=x_sb[:, g, c_tiles, :], in_=x_view[:, c_tiles, g * N_HALF : (g + 1) * N_HALF]
+                )
         nc.vector.tensor_copy(out=gamma_f32[:], in_=gamma_bf16[:])
 
         def flip(row_tiles):
@@ -103,12 +110,12 @@ def tile_selfattention_pb_kernel(tc, q, k, v, Wo, gamma, x, out):
                     )
             return bank
 
-        def regroup(copy, bank, name):
+        def regroup(copy, bank, name, order="p a r u"):
             tiles = bank.shape[1]
             grouped = work.tile([P, tiles * P * PACK], BF16, name=name, tag=name, align_bytes=64)
             copy(
-                out=grouped[:].bitcast(F32).rearrange("p (a r u) -> p a r u", a=tiles, u=HALVES),
-                in_=bank[:].rearrange("p a u r -> p a r u"),
+                out=grouped[:].bitcast(F32).rearrange("p (" + order[2:] + ") -> " + order, a=tiles, u=HALVES),
+                in_=bank[:].rearrange("p a u r -> " + order),
             )
             return grouped
 
@@ -118,18 +125,18 @@ def tile_selfattention_pb_kernel(tc, q, k, v, Wo, gamma, x, out):
         live = {}
 
         def flip_v(b):
-            bank = flip([v_rows[:, b * PAIR + a, :] for a in range(PAIR)])
-            live["v_grouped", b] = regroup(nc.scalar.copy, bank, "v_grouped")
+            bank = flip([v_rows[:, b, a, :] for a in range(PAIR)])
+            live["v_grouped", b] = regroup(nc.scalar.copy, bank, "v_grouped", "p r a u")
 
         def quantise_v(b):
             cols = slice(b * PAIR * P, (b + 1) * PAIR * P)
             quantise(live["v_grouped", b], v_codes[:, cols], v_scales[:, cols])
 
         def flip_wo(b):
-            live["wo_bank", b] = flip([wo_rows[:, b * PAIR + a, :] for a in range(PAIR)])
+            live["wo_bank", b] = flip([wo_rows[:, b, a, :] for a in range(PAIR)])
 
         def regroup_wo(b):
-            live["wo_grouped", b] = regroup(nc.vector.tensor_copy, live["wo_bank", b], "wo_grouped")
+            live["wo_grouped", b] = regroup(nc.vector.tensor_copy, live["wo_bank", b], "wo_grouped", "p r a u")
 
         def quantise_wo(b):
             cols = slice(b * PAIR * P, (b + 1) * PAIR * P)
@@ -229,7 +236,7 @@ def tile_selfattention_pb_kernel(tc, q, k, v, Wo, gamma, x, out):
                 live["y", i, h] = y_bank
 
         def finish(i):
-            a = i % GROUP
+            g, a = divmod(i, N_TILES // N_HALVES)
             for h in range(Y_BANKS):
                 c_tiles = slice(h * C_PER_BANK, (h + 1) * C_PER_BANK)
                 result = work.tile([P, C_PER_BANK, P], F32, name="result", bufs=6)
@@ -237,7 +244,7 @@ def tile_selfattention_pb_kernel(tc, q, k, v, Wo, gamma, x, out):
                     out=result[:],
                     in0=live["y", i, h][:],
                     scalar=gamma_f32[:, 0:1],
-                    in1=x_sb[:, i // GROUP, c_tiles, a * P : (a + 1) * P],
+                    in1=x_sb[:, g, c_tiles, a * P : (a + 1) * P],
                     op0=ALU.mult,
                     op1=ALU.add,
                 )

@@ -32,6 +32,10 @@ WO_PAIRS = C_TILES // PAIR
 Y_BANKS = 2
 C_PER_BANK = C_TILES // Y_BANKS
 
+Q_RUNS = ((0, 1), (1, 3), (4, 4), (8, 4), (12, 4))
+HEAD_WARM = 4
+WARM_ROUNDS = (1, 2, 3)
+
 FLOPS = 2 * N_POS * (D_QK * K_MX + K_MX * K_MX + C_OUT * K_MX)
 
 
@@ -47,7 +51,7 @@ def tile_selfattention_pb_kernel(tc, q, k, v, Wo, gamma, x, out):
 
     with ExitStack() as ctx:
         keep = ctx.enter_context(tc.tile_pool(name="keep", bufs=1))
-        work = ctx.enter_context(tc.tile_pool(name="work", bufs=3))
+        work = ctx.enter_context(tc.tile_pool(name="work", bufs=N_TILES))
         psum = ctx.enter_context(tc.psum_pool(name="psum", bufs=1))
 
         ident_bf16 = keep.tile([P, P], BF16, name="ident_bf16")
@@ -68,40 +72,50 @@ def tile_selfattention_pb_kernel(tc, q, k, v, Wo, gamma, x, out):
         row_sum = keep.tile([P, N_TILES], F32, name="row_sum")
         inv_sum = keep.tile([P, N_TILES], F32, name="inv_sum")
 
+        nc.scalar.dma_start(out=gamma_bf16[:], in_=gamma.partition_broadcast(P))
         warm_in = keep.tile([P, 1], F32, name="warm_in")
         warm_out = keep.tile([P, 1], F32, name="warm_out")
         nc.vector.memset(warm_in[:], 0.0)
         nc.scalar.activation(out=warm_out[:], in_=warm_in[:], func=ACT.Exp)
+        zeros = keep.tile([P, K_MX], BF16, name="zeros")
+        nc.vector.memset(zeros[:], 0.0)
         make_identity(nc, ident_bf16[:])
         make_identity(nc, ident_f32[:])
 
-        def load_q(g):
-            tiles = slice(g * GROUP, (g + 1) * GROUP)
+        def load_q(run):
+            first, count = Q_RUNS[run]
+            tiles = slice(first, first + count)
             nc.sync.dma_start(out=q_rows[:, tiles, :], in_=q_view[:, tiles, :])
 
         def load_pair(rows, view, b):
             nc.sync.dma_start(out=rows[:, b, :, :], in_=view[:, b, :, :])
 
-        nc.scalar.dma_start(out=gamma_bf16[:], in_=gamma.partition_broadcast(P))
         load_q(0)
         nc.sync.dma_start(out=k_sb[:], in_=k_view)
+        load_q(1)
         for b in range(V_PAIRS):
             load_pair(v_rows, v_view, b)
-        load_q(1)
+        load_q(2)
         for b in range(WO_PAIRS):
             load_pair(wo_rows, wo_view, b)
-        load_q(2)
         load_q(3)
+        load_q(4)
         for g in range(N_HALVES):
             for h in range(Y_BANKS):
                 c_tiles = slice(h * C_PER_BANK, (h + 1) * C_PER_BANK)
                 nc.sync.dma_start(
                     out=x_sb[:, g, c_tiles, :], in_=x_view[:, c_tiles, g * N_HALF : (g + 1) * N_HALF]
                 )
-        nc.vector.tensor_copy(out=gamma_f32[:], in_=gamma_bf16[:])
+        nc.gpsimd.tensor_copy(out=gamma_f32[:], in_=gamma_bf16[:])
 
-        def flip(row_tiles):
-            bank = psum.tile([P, len(row_tiles), HALVES, P], F32, name="flip_bank", tag="flip", bufs=3)
+        ctx.enter_context(tc.manual_schedule())
+
+        def keep_warm():
+            idle_bank = psum.tile([P, K_MX], F32, name="idle_bank", tag="attn", bufs=1)
+            nc.tensor.matmul(out=idle_bank[:], lhsT=zeros[:, 0:P], rhs=zeros[:], start=True, stop=True)
+
+        def flip(row_tiles, tag, bufs):
+            bank = psum.tile([P, len(row_tiles), HALVES, P], F32, name="flip_bank", tag=tag, bufs=bufs)
             for a, rows in enumerate(row_tiles):
                 words = rows.bitcast(F32)
                 for u in range(HALVES):
@@ -112,7 +126,9 @@ def tile_selfattention_pb_kernel(tc, q, k, v, Wo, gamma, x, out):
 
         def regroup(copy, bank, name, order="p a r u"):
             tiles = bank.shape[1]
-            grouped = work.tile([P, tiles * P * PACK], BF16, name=name, tag=name, align_bytes=64)
+            grouped = work.tile(
+                [P, tiles * P * PACK], BF16, name=name, tag=name, align_bytes=64, bufs=N_TILES if tiles == 1 else V_TILES
+            )
             copy(
                 out=grouped[:].bitcast(F32).rearrange("p (" + order[2:] + ") -> " + order, a=tiles, u=HALVES),
                 in_=bank[:].rearrange("p a u r -> " + order),
@@ -125,15 +141,18 @@ def tile_selfattention_pb_kernel(tc, q, k, v, Wo, gamma, x, out):
         live = {}
 
         def flip_v(b):
-            bank = flip([v_rows[:, b, a, :] for a in range(PAIR)])
-            live["v_grouped", b] = regroup(nc.scalar.copy, bank, "v_grouped", "p r a u")
+            live["v_bank", b] = flip([v_rows[:, b, a, :] for a in range(PAIR)], "proj", 3)
+
+        def regroup_v(b):
+            copy = nc.scalar.copy if b == 0 else nc.vector.tensor_copy
+            live["v_grouped", b] = regroup(copy, live["v_bank", b], "v_grouped", "p r a u")
 
         def quantise_v(b):
             cols = slice(b * PAIR * P, (b + 1) * PAIR * P)
             quantise(live["v_grouped", b], v_codes[:, cols], v_scales[:, cols])
 
         def flip_wo(b):
-            live["wo_bank", b] = flip([wo_rows[:, b, a, :] for a in range(PAIR)])
+            live["wo_bank", b] = flip([wo_rows[:, b, a, :] for a in range(PAIR)], "proj", 3)
 
         def regroup_wo(b):
             live["wo_grouped", b] = regroup(nc.vector.tensor_copy, live["wo_bank", b], "wo_grouped", "p r a u")
@@ -142,15 +161,20 @@ def tile_selfattention_pb_kernel(tc, q, k, v, Wo, gamma, x, out):
             cols = slice(b * PAIR * P, (b + 1) * PAIR * P)
             quantise(live["wo_grouped", b], wo_codes[:, cols], wo_scales[:, cols])
 
-        def flip_q(g):
-            bank = psum.tile([P, GROUP, P], BF16, name="q_bank", tag="flip", bufs=3)
-            for a in range(GROUP):
+        def flip_q(run):
+            first, count = Q_RUNS[run]
+            bank = psum.tile([P, count, P], BF16, name="q_bank", tag="proj", bufs=3)
+            for a in range(count):
                 nc.tensor.transpose(
-                    out=bank[:, a, :], in_=q_rows[:, g * GROUP + a, :], identity=ident_bf16[:]
+                    out=bank[:, a, :], in_=q_rows[:, first + a, :], identity=ident_bf16[:]
                 )
+            live["q_bank", run] = bank
+
+        def copy_q(run):
+            first, count = Q_RUNS[run]
             nc.scalar.copy(
-                out=q_flipped[:, g * GROUP * P : (g + 1) * GROUP * P],
-                in_=bank[:].rearrange("p a r -> p (a r)"),
+                out=q_flipped[:, first * P : (first + count) * P],
+                in_=live["q_bank", run][:].rearrange("p a r -> p (a r)"),
             )
 
         def scores(i):
@@ -182,7 +206,10 @@ def tile_selfattention_pb_kernel(tc, q, k, v, Wo, gamma, x, out):
             live["e_rows", i] = e_rows
 
         def flip_e(i):
-            live["e_grouped", i] = regroup(nc.scalar.copy, flip([live["e_rows", i][:]]), "e_grouped")
+            live["e_bank", i] = flip([live["e_rows", i][:]], "flip", 2)
+
+        def regroup_e(i):
+            live["e_grouped", i] = regroup(nc.scalar.copy, live["e_bank", i], "e_grouped")
 
         def quantise_e(i):
             e_codes = work.tile([P, P], U32, name="e_codes", align_bytes=64)
@@ -203,14 +230,20 @@ def tile_selfattention_pb_kernel(tc, q, k, v, Wo, gamma, x, out):
                 start=True,
                 stop=True,
             )
+            live["attn", i] = attn_bank
+
+        def divide(i):
             o_rows = work.tile([P, K_MX], BF16, name="o_rows")
             nc.scalar.activation(
-                out=o_rows[:], in_=attn_bank[:], func=ACT.Copy, scale=inv_sum[:, i : i + 1]
+                out=o_rows[:], in_=live["attn", i][:], func=ACT.Copy, scale=inv_sum[:, i : i + 1]
             )
             live["o_rows", i] = o_rows
 
         def flip_o(i):
-            live["o_grouped", i] = regroup(nc.scalar.copy, flip([live["o_rows", i][:]]), "o_grouped")
+            live["o_bank", i] = flip([live["o_rows", i][:]], "flip", 2)
+
+        def regroup_o(i):
+            live["o_grouped", i] = regroup(nc.scalar.copy, live["o_bank", i], "o_grouped")
 
         def quantise_o(i):
             o_codes = work.tile([P, P], U32, name="o_codes", align_bytes=64)
@@ -219,58 +252,74 @@ def tile_selfattention_pb_kernel(tc, q, k, v, Wo, gamma, x, out):
             live["o_codes", i] = o_codes
             live["o_scales", i] = o_scales
 
-        def project(i):
-            for h in range(Y_BANKS):
-                y_bank = psum.tile([P, C_PER_BANK, P], F32, name="y_bank", tag="proj", bufs=2)
-                for j in range(C_PER_BANK):
-                    cols = slice((h * C_PER_BANK + j) * P, (h * C_PER_BANK + j + 1) * P)
-                    nc.tensor.matmul_mx(
-                        out=y_bank[:, j, :],
-                        lhsT=wo_codes[:, cols].bitcast(FP8X4),
-                        lhsT_scale=wo_scales[:, cols],
-                        rhs=live["o_codes", i][:].bitcast(FP8X4),
-                        rhs_scale=live["o_scales", i][:],
-                        start=True,
-                        stop=True,
-                    )
-                live["y", i, h] = y_bank
-
-        def finish(i):
-            g, a = divmod(i, N_TILES // N_HALVES)
-            for h in range(Y_BANKS):
-                c_tiles = slice(h * C_PER_BANK, (h + 1) * C_PER_BANK)
-                result = work.tile([P, C_PER_BANK, P], F32, name="result", bufs=6)
-                nc.vector.scalar_tensor_tensor(
-                    out=result[:],
-                    in0=live["y", i, h][:],
-                    scalar=gamma_f32[:, 0:1],
-                    in1=x_sb[:, g, c_tiles, a * P : (a + 1) * P],
-                    op0=ALU.mult,
-                    op1=ALU.add,
+        def project(i, h):
+            y_bank = psum.tile([P, C_PER_BANK, P], F32, name="y_bank", tag="proj", bufs=3)
+            for j in range(C_PER_BANK):
+                cols = slice((h * C_PER_BANK + j) * P, (h * C_PER_BANK + j + 1) * P)
+                nc.tensor.matmul_mx(
+                    out=y_bank[:, j, :],
+                    lhsT=wo_codes[:, cols].bitcast(FP8X4),
+                    lhsT_scale=wo_scales[:, cols],
+                    rhs=live["o_codes", i][:].bitcast(FP8X4),
+                    rhs_scale=live["o_scales", i][:],
+                    start=True,
+                    stop=True,
                 )
-                nc.sync.dma_start(out=out_view[:, c_tiles, i * P : (i + 1) * P], in_=result[:])
+            live["y", i, h] = y_bank
 
-        def stage(step, i, count):
+        def finish(i, h):
+            g, a = divmod(i, N_TILES // N_HALVES)
+            c_tiles = slice(h * C_PER_BANK, (h + 1) * C_PER_BANK)
+            result = work.tile([P, C_PER_BANK, P], F32, name="result", bufs=Y_BANKS * N_TILES)
+            nc.vector.scalar_tensor_tensor(
+                out=result[:],
+                in0=live["y", i, h][:],
+                scalar=gamma_f32[:, 0:1],
+                in1=x_sb[:, g, c_tiles, a * P : (a + 1) * P],
+                op0=ALU.mult,
+                op1=ALU.add,
+            )
+            nc.sync.dma_start(out=out_view[:, c_tiles, i * P : (i + 1) * P], in_=result[:])
+
+        def stage(step, i, count, *more):
             if 0 <= i < count:
-                step(i)
+                step(i, *more)
 
+        for step in range(HEAD_WARM):
+            keep_warm()
         flip_q(0)
-        scores(0)
-        for c in range(N_TILES + 6):
-            stage(project, c - 6, N_TILES)
+        copy_q(0)
+        for c in range(N_TILES + 10):
+            w = c - 2
+            stage(project, c - 10, N_TILES, 0)
+            stage(finish, c - 10, N_TILES, 0)
+            if c == 1:
+                flip_q(1)
+                copy_q(1)
+            stage(scores, c, N_TILES)
+            if w in WARM_ROUNDS:
+                keep_warm()
+            if w == 0:
+                flip_v(0)
+                flip_v(1)
+            stage(flip_o, c - 8, N_TILES)
+            stage(divide, c - 7, N_TILES)
+            stage(flip_e, c - 4, N_TILES)
+            stage(regroup_wo, w - 3, WO_PAIRS)
+            if w in (0, 2, 4):
+                flip_q(2 + w // 2)
+            stage(project, c - 10, N_TILES, 1)
             stage(row_maximum, c, N_TILES)
-            stage(regroup_wo, c - 2, WO_PAIRS)
-            stage(quantise_e, c - 2, N_TILES)
-            stage(quantise_o, c - 5, N_TILES)
-            stage(finish, c - 6, N_TILES)
-            stage(exponentials, c, N_TILES)
-            stage(attend, c - 3, N_TILES)
-            stage(flip_e, c - 1, N_TILES)
-            stage(flip_o, c - 4, N_TILES)
-            stage(scores, c + 1, N_TILES)
-            stage(flip_v, c, V_PAIRS)
-            stage(flip_wo, c - 1, WO_PAIRS)
-            if c % GROUP == 1:
-                stage(flip_q, c // GROUP + 1, N_GROUPS)
-            stage(quantise_v, c - 1, V_PAIRS)
-            stage(quantise_wo, c - 2, WO_PAIRS)
+            stage(quantise_e, c - 5, N_TILES)
+            stage(quantise_v, w - 2, V_PAIRS)
+            stage(exponentials, c - 1, N_TILES)
+            stage(regroup_o, c - 8, N_TILES)
+            stage(attend, c - 6, N_TILES)
+            stage(flip_wo, w - 2, WO_PAIRS)
+            stage(finish, c - 10, N_TILES, 1)
+            stage(quantise_wo, w - 4, WO_PAIRS)
+            stage(quantise_o, c - 8, N_TILES)
+            stage(regroup_v, w, V_PAIRS)
+            if w in (1, 3, 5):
+                copy_q(2 + w // 2)
+            stage(regroup_e, c - 4, N_TILES)

@@ -29,12 +29,13 @@ N_HALF = N_POS // N_HALVES
 PAIR = 2
 V_PAIRS = V_TILES // PAIR
 WO_PAIRS = C_TILES // PAIR
-Y_BANKS = 2
+N_PAIRS = N_TILES // PAIR
+Y_BANKS = 4
 C_PER_BANK = C_TILES // Y_BANKS
+W = PAIR * P
 
 Q_RUNS = ((0, 1), (1, 3), (4, 4), (8, 4), (12, 4))
 HEAD_WARM = 4
-WARM_ROUNDS = (1, 2, 3)
 
 FLOPS = 2 * N_POS * (D_QK * K_MX + K_MX * K_MX + C_OUT * K_MX)
 
@@ -101,8 +102,8 @@ def tile_selfattention_pb_kernel(tc, q, k, v, Wo, gamma, x, out):
         load_q(3)
         load_q(4)
         for g in range(N_HALVES):
-            for h in range(Y_BANKS):
-                c_tiles = slice(h * C_PER_BANK, (h + 1) * C_PER_BANK)
+            for h in range(N_HALVES):
+                c_tiles = slice(h * C_TILES // N_HALVES, (h + 1) * C_TILES // N_HALVES)
                 nc.sync.dma_start(
                     out=x_sb[:, g, c_tiles, :], in_=x_view[:, c_tiles, g * N_HALF : (g + 1) * N_HALF]
                 )
@@ -124,10 +125,10 @@ def tile_selfattention_pb_kernel(tc, q, k, v, Wo, gamma, x, out):
                     )
             return bank
 
-        def regroup(copy, bank, name, order="p a r u"):
+        def regroup(copy, bank, name, bufs, order="p a r u"):
             tiles = bank.shape[1]
             grouped = work.tile(
-                [P, tiles * P * PACK], BF16, name=name, tag=name, align_bytes=64, bufs=N_TILES if tiles == 1 else V_TILES
+                [P, tiles * P * PACK], BF16, name=name, tag=name, align_bytes=64, bufs=bufs
             )
             copy(
                 out=grouped[:].bitcast(F32).rearrange("p (" + order[2:] + ") -> " + order, a=tiles, u=HALVES),
@@ -144,8 +145,7 @@ def tile_selfattention_pb_kernel(tc, q, k, v, Wo, gamma, x, out):
             live["v_bank", b] = flip([v_rows[:, b, a, :] for a in range(PAIR)], "proj", 3)
 
         def regroup_v(b):
-            copy = nc.scalar.copy if b == 0 else nc.vector.tensor_copy
-            live["v_grouped", b] = regroup(copy, live["v_bank", b], "v_grouped", "p r a u")
+            live["v_grouped", b] = regroup(nc.vector.tensor_copy, live["v_bank", b], "v_grouped", V_PAIRS, "p r a u")
 
         def quantise_v(b):
             cols = slice(b * PAIR * P, (b + 1) * PAIR * P)
@@ -155,7 +155,8 @@ def tile_selfattention_pb_kernel(tc, q, k, v, Wo, gamma, x, out):
             live["wo_bank", b] = flip([wo_rows[:, b, a, :] for a in range(PAIR)], "proj", 3)
 
         def regroup_wo(b):
-            live["wo_grouped", b] = regroup(nc.vector.tensor_copy, live["wo_bank", b], "wo_grouped", "p r a u")
+            copy = nc.scalar.copy if b == 0 else nc.vector.tensor_copy
+            live["wo_grouped", b] = regroup(copy, live["wo_bank", b], "wo_grouped", WO_PAIRS, "p r a u")
 
         def quantise_wo(b):
             cols = slice(b * PAIR * P, (b + 1) * PAIR * P)
@@ -178,7 +179,7 @@ def tile_selfattention_pb_kernel(tc, q, k, v, Wo, gamma, x, out):
             )
 
         def scores(i):
-            s_bank = psum.tile([P, K_MX], F32, name="s_bank", tag="scores", bufs=2)
+            s_bank = psum.tile([P, K_MX], F32, name="s_bank", tag="scores", bufs=3)
             nc.tensor.matmul(
                 out=s_bank[:], lhsT=q_flipped[:, i * P : (i + 1) * P], rhs=k_sb[:], start=True, stop=True
             )
@@ -205,26 +206,29 @@ def tile_selfattention_pb_kernel(tc, q, k, v, Wo, gamma, x, out):
             )
             live["e_rows", i] = e_rows
 
-        def flip_e(i):
-            live["e_bank", i] = flip([live["e_rows", i][:]], "flip", 2)
+        def flip_e(p):
+            live["e_bank", p] = flip([live["e_rows", PAIR * p + a][:] for a in range(PAIR)], "flip", 1)
 
-        def regroup_e(i):
-            live["e_grouped", i] = regroup(nc.scalar.copy, live["e_bank", i], "e_grouped")
+        def regroup_e(p):
+            live["e_grouped", p] = regroup(nc.scalar.copy, live["e_bank", p], "e_grouped", N_PAIRS)
 
-        def quantise_e(i):
-            e_codes = work.tile([P, P], U32, name="e_codes", align_bytes=64)
-            e_scales = work.tile([P, P], U8, name="e_scales", align_bytes=64)
-            quantise(live["e_grouped", i], e_codes[:], e_scales[:])
-            live["e_codes", i] = e_codes
-            live["e_scales", i] = e_scales
-            nc.vector.reciprocal(out=inv_sum[:, i : i + 1], in_=row_sum[:, i : i + 1])
+        def quantise_e(p):
+            e_codes = work.tile([P, W], U32, name="e_codes", align_bytes=64, bufs=N_PAIRS)
+            e_scales = work.tile([P, W], U8, name="e_scales", align_bytes=64, bufs=N_PAIRS)
+            quantise(live["e_grouped", p], e_codes[:], e_scales[:])
+            live["e_codes", p] = e_codes
+            live["e_scales", p] = e_scales
+            tiles = slice(PAIR * p, PAIR * (p + 1))
+            nc.vector.reciprocal(out=inv_sum[:, tiles], in_=row_sum[:, tiles])
 
         def attend(i):
             attn_bank = psum.tile([P, K_MX], F32, name="attn_bank", tag="attn", bufs=1)
+            p, a = divmod(i, PAIR)
+            cols = slice(a * P, (a + 1) * P)
             nc.tensor.matmul_mx(
                 out=attn_bank[:],
-                lhsT=live["e_codes", i][:].bitcast(FP8X4),
-                lhsT_scale=live["e_scales", i][:],
+                lhsT=live["e_codes", p][:, cols].bitcast(FP8X4),
+                lhsT_scale=live["e_scales", p][:, cols],
                 rhs=v_codes[:].bitcast(FP8X4),
                 rhs_scale=v_scales[:],
                 start=True,
@@ -239,87 +243,103 @@ def tile_selfattention_pb_kernel(tc, q, k, v, Wo, gamma, x, out):
             )
             live["o_rows", i] = o_rows
 
-        def flip_o(i):
-            live["o_bank", i] = flip([live["o_rows", i][:]], "flip", 2)
+        def flip_o(p):
+            live["o_bank", p] = flip([live["o_rows", PAIR * p + a][:] for a in range(PAIR)], "flip", 1)
 
-        def regroup_o(i):
-            live["o_grouped", i] = regroup(nc.scalar.copy, live["o_bank", i], "o_grouped")
+        def regroup_o(p):
+            live["o_grouped", p] = regroup(nc.scalar.copy, live["o_bank", p], "o_grouped", N_PAIRS)
 
-        def quantise_o(i):
-            o_codes = work.tile([P, P], U32, name="o_codes", align_bytes=64)
-            o_scales = work.tile([P, P], U8, name="o_scales", align_bytes=64)
-            quantise(live["o_grouped", i], o_codes[:], o_scales[:])
-            live["o_codes", i] = o_codes
-            live["o_scales", i] = o_scales
+        def quantise_o(p):
+            o_codes = work.tile([P, W], U32, name="o_codes", align_bytes=64, bufs=N_PAIRS)
+            o_scales = work.tile([P, W], U8, name="o_scales", align_bytes=64, bufs=N_PAIRS)
+            quantise(live["o_grouped", p], o_codes[:], o_scales[:])
+            live["o_codes", p] = o_codes
+            live["o_scales", p] = o_scales
 
-        def project(i, h):
-            y_bank = psum.tile([P, C_PER_BANK, P], F32, name="y_bank", tag="proj", bufs=3)
+        def project(p, h):
+            y_bank = psum.tile([P, C_PER_BANK, W], F32, name="y_bank", tag="proj", bufs=3)
             for j in range(C_PER_BANK):
                 cols = slice((h * C_PER_BANK + j) * P, (h * C_PER_BANK + j + 1) * P)
                 nc.tensor.matmul_mx(
                     out=y_bank[:, j, :],
                     lhsT=wo_codes[:, cols].bitcast(FP8X4),
                     lhsT_scale=wo_scales[:, cols],
-                    rhs=live["o_codes", i][:].bitcast(FP8X4),
-                    rhs_scale=live["o_scales", i][:],
+                    rhs=live["o_codes", p][:].bitcast(FP8X4),
+                    rhs_scale=live["o_scales", p][:],
                     start=True,
                     stop=True,
                 )
-            live["y", i, h] = y_bank
+            live["y", p, h] = y_bank
 
-        def finish(i, h):
-            g, a = divmod(i, N_TILES // N_HALVES)
+        def finish(p, h):
+            g, a = divmod(p, N_PAIRS // N_HALVES)
             c_tiles = slice(h * C_PER_BANK, (h + 1) * C_PER_BANK)
-            result = work.tile([P, C_PER_BANK, P], F32, name="result", bufs=Y_BANKS * N_TILES)
+            result = work.tile([P, C_PER_BANK, W], F32, name="result", bufs=Y_BANKS * N_PAIRS)
             nc.vector.scalar_tensor_tensor(
                 out=result[:],
-                in0=live["y", i, h][:],
+                in0=live["y", p, h][:],
                 scalar=gamma_f32[:, 0:1],
-                in1=x_sb[:, g, c_tiles, a * P : (a + 1) * P],
+                in1=x_sb[:, g, c_tiles, a * W : (a + 1) * W],
                 op0=ALU.mult,
                 op1=ALU.add,
             )
-            nc.sync.dma_start(out=out_view[:, c_tiles, i * P : (i + 1) * P], in_=result[:])
+            nc.sync.dma_start(out=out_view[:, c_tiles, p * W : (p + 1) * W], in_=result[:])
 
-        def stage(step, i, count, *more):
-            if 0 <= i < count:
-                step(i, *more)
+        def tile_step(step, i):
+            if 0 <= i < N_TILES:
+                step(i)
+
+        def pair_step(step, i, *more):
+            if 0 <= i < N_TILES and i % PAIR == PAIR - 1:
+                step(i // PAIR, *more)
 
         for step in range(HEAD_WARM):
             keep_warm()
         flip_q(0)
         copy_q(0)
-        for c in range(N_TILES + 10):
-            w = c - 2
-            stage(project, c - 10, N_TILES, 0)
-            stage(finish, c - 10, N_TILES, 0)
-            if c == 1:
-                flip_q(1)
-                copy_q(1)
-            stage(scores, c, N_TILES)
-            if w in WARM_ROUNDS:
-                keep_warm()
-            if w == 0:
-                flip_v(0)
-                flip_v(1)
-            stage(flip_o, c - 8, N_TILES)
-            stage(divide, c - 7, N_TILES)
-            stage(flip_e, c - 4, N_TILES)
-            stage(regroup_wo, w - 3, WO_PAIRS)
-            if w in (0, 2, 4):
-                flip_q(2 + w // 2)
-            stage(project, c - 10, N_TILES, 1)
-            stage(row_maximum, c, N_TILES)
-            stage(quantise_e, c - 5, N_TILES)
-            stage(quantise_v, w - 2, V_PAIRS)
-            stage(exponentials, c - 1, N_TILES)
-            stage(regroup_o, c - 8, N_TILES)
-            stage(attend, c - 6, N_TILES)
-            stage(flip_wo, w - 2, WO_PAIRS)
-            stage(finish, c - 10, N_TILES, 1)
-            stage(quantise_wo, w - 4, WO_PAIRS)
-            stage(quantise_o, c - 8, N_TILES)
-            stage(regroup_v, w, V_PAIRS)
-            if w in (1, 3, 5):
-                copy_q(2 + w // 2)
-            stage(regroup_e, c - 4, N_TILES)
+        scores(0)
+        flip_q(1)
+        copy_q(1)
+        for c in range(N_TILES + 14):
+            if c in (6, 7):
+                quantise_v(c - 6)
+            tile_step(exponentials, c - 3)
+            pair_step(finish, c - 14, 3)
+            pair_step(project, c - 12, 2)
+            pair_step(quantise_o, c - 11)
+            pair_step(quantise_e, c - 6)
+            pair_step(flip_e, c - 4)
+            if c in (3, 5, 7, 9):
+                flip_wo((c - 3) // 2)
+            if c in (3, 7):
+                copy_q(2 if c == 3 else 3)
+            if c == 7:
+                copy_q(4)
+            tile_step(divide, c - 8)
+            pair_step(finish, c - 12, 0)
+            if c in (4, 6, 8, 10):
+                regroup_wo((c - 4) // 2)
+            pair_step(project, c - 12, 3)
+            if c == 2:
+                flip_q(2)
+            if c == 6:
+                flip_q(3)
+                flip_q(4)
+            pair_step(finish, c - 13, 2)
+            pair_step(project, c - 11, 0)
+            if c in (0, 1):
+                flip_v(c)
+            pair_step(flip_o, c - 9)
+            pair_step(project, c - 11, 1)
+            if c in (2, 4):
+                regroup_v((c - 2) // 2)
+            pair_step(regroup_o, c - 9)
+            if c > 0:
+                tile_step(scores, c)
+            if c == 10:
+                for b in range(WO_PAIRS):
+                    quantise_wo(b)
+            pair_step(regroup_e, c - 4)
+            pair_step(finish, c - 12, 1)
+            tile_step(row_maximum, c - 1)
+            tile_step(attend, c - 7)

@@ -35,7 +35,10 @@ C_PER_BANK = C_TILES // Y_BANKS
 W = PAIR * P
 
 Q_RUNS = ((0, 1), (1, 3), (4, 4), (8, 4), (12, 4))
-HEAD_WARM = 4
+HEAD_WARM = 3
+
+SPARE_TILE = 5
+SPARE_PAIR = 3
 
 FLOPS = 2 * N_POS * (D_QK * K_MX + K_MX * K_MX + C_OUT * K_MX)
 
@@ -179,7 +182,8 @@ def tile_selfattention_pb_kernel(tc, q, k, v, Wo, gamma, x, out):
             )
 
         def scores(i):
-            s_bank = psum.tile([P, K_MX], F32, name="s_bank", tag="scores", bufs=3)
+            tag = "proj" if i == SPARE_TILE else "scores"
+            s_bank = psum.tile([P, K_MX], F32, name="s_bank", tag=tag, bufs=3)
             nc.tensor.matmul(
                 out=s_bank[:], lhsT=q_flipped[:, i * P : (i + 1) * P], rhs=k_sb[:], start=True, stop=True
             )
@@ -257,7 +261,8 @@ def tile_selfattention_pb_kernel(tc, q, k, v, Wo, gamma, x, out):
             live["o_scales", p] = o_scales
 
         def project(p, h):
-            y_bank = psum.tile([P, C_PER_BANK, W], F32, name="y_bank", tag="proj", bufs=3)
+            tag = "scores" if h == 2 and p >= SPARE_PAIR else "proj"
+            y_bank = psum.tile([P, C_PER_BANK, W], F32, name="y_bank", tag=tag, bufs=3)
             for j in range(C_PER_BANK):
                 cols = slice((h * C_PER_BANK + j) * P, (h * C_PER_BANK + j + 1) * P)
                 nc.tensor.matmul_mx(
@@ -300,46 +305,44 @@ def tile_selfattention_pb_kernel(tc, q, k, v, Wo, gamma, x, out):
         scores(0)
         flip_q(1)
         copy_q(1)
-        for c in range(N_TILES + 14):
-            if c in (6, 7):
-                quantise_v(c - 6)
-            tile_step(exponentials, c - 3)
-            pair_step(finish, c - 14, 3)
-            pair_step(project, c - 12, 2)
+        for c in range(N_TILES + 13):
             pair_step(quantise_o, c - 11)
-            pair_step(quantise_e, c - 6)
+            pair_step(finish, c - 13, 1)
+            pair_step(project, c - 12, 1)
+            pair_step(project, c - 11, 2)
+            if c in (1, 3):
+                flip_v(c // 2)
+            tile_step(exponentials, c - 3)
+            tile_step(divide, c - 8)
+            pair_step(project, c - 11, 3)
+            pair_step(flip_o, c - 9)
+            pair_step(finish, c - 12, 3)
+            if c in (4, 6, 8, 10):
+                regroup_wo(c // 2 - 2)
+            pair_step(finish, c - 12, 2)
             pair_step(flip_e, c - 4)
             if c in (3, 5, 7, 9):
-                flip_wo((c - 3) // 2)
-            if c in (3, 7):
-                copy_q(2 if c == 3 else 3)
-            if c == 7:
-                copy_q(4)
-            tile_step(divide, c - 8)
-            pair_step(finish, c - 12, 0)
-            if c in (4, 6, 8, 10):
-                regroup_wo((c - 4) // 2)
-            pair_step(project, c - 12, 3)
-            if c == 2:
-                flip_q(2)
-            if c == 6:
-                flip_q(3)
-                flip_q(4)
-            pair_step(finish, c - 13, 2)
-            pair_step(project, c - 11, 0)
-            if c in (0, 1):
-                flip_v(c)
-            pair_step(flip_o, c - 9)
-            pair_step(project, c - 11, 1)
+                flip_wo(c // 2 - 1)
+            if c in (3, 6, 8):
+                copy_q((c + 1) // 2)
+            pair_step(project, c - 12, 0)
             if c in (2, 4):
-                regroup_v((c - 2) // 2)
-            pair_step(regroup_o, c - 9)
-            if c > 0:
-                tile_step(scores, c)
+                regroup_v(c // 2 - 1)
+            if c == 5:
+                quantise_v(0)
+                quantise_v(1)
+            pair_step(regroup_e, c - 4)
+            if c in (2, 5, 7):
+                flip_q(c // 2 + 1)
+            tile_step(row_maximum, c - 1)
+            if c == 1:
+                keep_warm()
             if c == 10:
                 for b in range(WO_PAIRS):
                     quantise_wo(b)
-            pair_step(regroup_e, c - 4)
-            pair_step(finish, c - 12, 1)
-            tile_step(row_maximum, c - 1)
+            if c > 0:
+                tile_step(scores, c)
+            pair_step(finish, c - 13, 0)
+            pair_step(regroup_o, c - 9)
             tile_step(attend, c - 7)
+            pair_step(quantise_e, c - 5)

@@ -307,42 +307,42 @@ def tile_selfattention_pb_kernel(tc, q, k, v, Wo, gamma, x, out):
         copy_q(1)
         for c in range(N_TILES + 13):
             pair_step(quantise_o, c - 11)
-            pair_step(finish, c - 13, 1)
             pair_step(project, c - 12, 1)
-            pair_step(project, c - 11, 2)
             if c in (1, 3):
                 flip_v(c // 2)
+            pair_step(finish, c - 13, 1)
+            if c in (2, 4):
+                regroup_v(c // 2 - 1)
             tile_step(exponentials, c - 3)
             tile_step(divide, c - 8)
+            pair_step(flip_e, c - 4)
             pair_step(project, c - 11, 3)
+            if c == 5:
+                quantise_v(0)
+                quantise_v(1)
             pair_step(flip_o, c - 9)
+            pair_step(project, c - 11, 2)
             pair_step(finish, c - 12, 3)
             if c in (4, 6, 8, 10):
                 regroup_wo(c // 2 - 2)
             pair_step(finish, c - 12, 2)
-            pair_step(flip_e, c - 4)
             if c in (3, 5, 7, 9):
                 flip_wo(c // 2 - 1)
             if c in (3, 6, 8):
                 copy_q((c + 1) // 2)
             pair_step(project, c - 12, 0)
-            if c in (2, 4):
-                regroup_v(c // 2 - 1)
-            if c == 5:
-                quantise_v(0)
-                quantise_v(1)
             pair_step(regroup_e, c - 4)
+            pair_step(finish, c - 13, 0)
             if c in (2, 5, 7):
                 flip_q(c // 2 + 1)
             tile_step(row_maximum, c - 1)
-            if c == 1:
+            if c in (1, 5):
                 keep_warm()
             if c == 10:
                 for b in range(WO_PAIRS):
                     quantise_wo(b)
             if c > 0:
                 tile_step(scores, c)
-            pair_step(finish, c - 13, 0)
             pair_step(regroup_o, c - 9)
-            tile_step(attend, c - 7)
             pair_step(quantise_e, c - 5)
+            tile_step(attend, c - 7)

@@ -72,6 +72,8 @@ def tile_selfattention_pb_kernel(tc, q, k, v, Wo, gamma, x, out):
         v_scales = keep.tile([P, K_MX], U8, name="v_scales", align_bytes=64)
         wo_codes = keep.tile([P, C_OUT], U32, name="wo_codes", align_bytes=64)
         wo_scales = keep.tile([P, C_OUT], U8, name="wo_scales", align_bytes=64)
+        v_grouped = keep.tile([P, V_TILES * P * PACK], BF16, name="v_grouped", align_bytes=64)
+        wo_grouped = keep.tile([P, C_TILES * P * PACK], BF16, name="wo_grouped", align_bytes=64)
         neg_max = keep.tile([P, N_TILES], F32, name="neg_max")
         row_sum = keep.tile([P, N_TILES], F32, name="row_sum")
         inv_sum = keep.tile([P, N_TILES], F32, name="inv_sum")
@@ -128,19 +130,14 @@ def tile_selfattention_pb_kernel(tc, q, k, v, Wo, gamma, x, out):
                     )
             return bank
 
-        def regroup(copy, bank, name, bufs, order="p a r u"):
-            tiles = bank.shape[1]
-            grouped = work.tile(
-                [P, tiles * P * PACK], BF16, name=name, tag=name, align_bytes=64, bufs=bufs
-            )
+        def regroup(copy, bank, grouped, order="p a r u"):
             copy(
-                out=grouped[:].bitcast(F32).rearrange("p (" + order[2:] + ") -> " + order, a=tiles, u=HALVES),
+                out=grouped.bitcast(F32).rearrange("p (" + order[2:] + ") -> " + order, a=PAIR, u=HALVES),
                 in_=bank[:].rearrange("p a u r -> " + order),
             )
-            return grouped
 
         def quantise(grouped, codes, scales):
-            nc.vector.quantize_mx(out=codes.bitcast(FP8X4), scales=scales, in_=grouped[:])
+            nc.vector.quantize_mx(out=codes.bitcast(FP8X4), scales=scales, in_=grouped)
 
         live = {}
 
@@ -148,22 +145,22 @@ def tile_selfattention_pb_kernel(tc, q, k, v, Wo, gamma, x, out):
             live["v_bank", b] = flip([v_rows[:, b, a, :] for a in range(PAIR)], "proj", 3)
 
         def regroup_v(b):
-            live["v_grouped", b] = regroup(nc.vector.tensor_copy, live["v_bank", b], "v_grouped", V_PAIRS, "p r a u")
+            part = slice(b * W * PACK, (b + 1) * W * PACK)
+            regroup(nc.vector.tensor_copy, live["v_bank", b], v_grouped[:, part], "p r a u")
 
-        def quantise_v(b):
-            cols = slice(b * PAIR * P, (b + 1) * PAIR * P)
-            quantise(live["v_grouped", b], v_codes[:, cols], v_scales[:, cols])
+        def quantise_v():
+            quantise(v_grouped[:], v_codes[:], v_scales[:])
 
         def flip_wo(b):
             live["wo_bank", b] = flip([wo_rows[:, b, a, :] for a in range(PAIR)], "proj", 3)
 
         def regroup_wo(b):
             copy = nc.scalar.copy if b == 0 else nc.vector.tensor_copy
-            live["wo_grouped", b] = regroup(copy, live["wo_bank", b], "wo_grouped", WO_PAIRS, "p r a u")
+            part = slice(b * W * PACK, (b + 1) * W * PACK)
+            regroup(copy, live["wo_bank", b], wo_grouped[:, part], "p r a u")
 
-        def quantise_wo(b):
-            cols = slice(b * PAIR * P, (b + 1) * PAIR * P)
-            quantise(live["wo_grouped", b], wo_codes[:, cols], wo_scales[:, cols])
+        def quantise_wo():
+            quantise(wo_grouped[:], wo_codes[:], wo_scales[:])
 
         def flip_q(run):
             first, count = Q_RUNS[run]
@@ -214,12 +211,14 @@ def tile_selfattention_pb_kernel(tc, q, k, v, Wo, gamma, x, out):
             live["e_bank", p] = flip([live["e_rows", PAIR * p + a][:] for a in range(PAIR)], "flip", 1)
 
         def regroup_e(p):
-            live["e_grouped", p] = regroup(nc.scalar.copy, live["e_bank", p], "e_grouped", N_PAIRS)
+            grouped = work.tile([P, W * PACK], BF16, name="e_grouped", align_bytes=64, bufs=N_PAIRS)
+            regroup(nc.scalar.copy, live["e_bank", p], grouped[:])
+            live["e_grouped", p] = grouped
 
         def quantise_e(p):
             e_codes = work.tile([P, W], U32, name="e_codes", align_bytes=64, bufs=N_PAIRS)
             e_scales = work.tile([P, W], U8, name="e_scales", align_bytes=64, bufs=N_PAIRS)
-            quantise(live["e_grouped", p], e_codes[:], e_scales[:])
+            quantise(live["e_grouped", p][:], e_codes[:], e_scales[:])
             live["e_codes", p] = e_codes
             live["e_scales", p] = e_scales
             tiles = slice(PAIR * p, PAIR * (p + 1))
@@ -251,12 +250,14 @@ def tile_selfattention_pb_kernel(tc, q, k, v, Wo, gamma, x, out):
             live["o_bank", p] = flip([live["o_rows", PAIR * p + a][:] for a in range(PAIR)], "flip", 1)
 
         def regroup_o(p):
-            live["o_grouped", p] = regroup(nc.scalar.copy, live["o_bank", p], "o_grouped", N_PAIRS)
+            grouped = work.tile([P, W * PACK], BF16, name="o_grouped", align_bytes=64, bufs=N_PAIRS)
+            regroup(nc.scalar.copy, live["o_bank", p], grouped[:])
+            live["o_grouped", p] = grouped
 
         def quantise_o(p):
             o_codes = work.tile([P, W], U32, name="o_codes", align_bytes=64, bufs=N_PAIRS)
             o_scales = work.tile([P, W], U8, name="o_scales", align_bytes=64, bufs=N_PAIRS)
-            quantise(live["o_grouped", p], o_codes[:], o_scales[:])
+            quantise(live["o_grouped", p][:], o_codes[:], o_scales[:])
             live["o_codes", p] = o_codes
             live["o_scales", p] = o_scales
 
@@ -280,15 +281,21 @@ def tile_selfattention_pb_kernel(tc, q, k, v, Wo, gamma, x, out):
             g, a = divmod(p, N_PAIRS // N_HALVES)
             c_tiles = slice(h * C_PER_BANK, (h + 1) * C_PER_BANK)
             result = work.tile([P, C_PER_BANK, W], F32, name="result", bufs=Y_BANKS * N_PAIRS)
-            nc.vector.scalar_tensor_tensor(
-                out=result[:],
-                in0=live["y", p, h][:],
-                scalar=gamma_f32[:, 0:1],
-                in1=x_sb[:, g, c_tiles, a * W : (a + 1) * W],
-                op0=ALU.mult,
-                op1=ALU.add,
-            )
-            nc.sync.dma_start(out=out_view[:, c_tiles, p * W : (p + 1) * W], in_=result[:])
+            x_part = x_sb[:, g, c_tiles, a * W : (a + 1) * W]
+            out_part = out_view[:, c_tiles, p * W : (p + 1) * W]
+            pieces = C_PER_BANK if (p, h) == (N_PAIRS - 1, 0) else 1
+            step = C_PER_BANK // pieces
+            for j in range(0, C_PER_BANK, step):
+                rows = slice(j, j + step)
+                nc.vector.scalar_tensor_tensor(
+                    out=result[:, rows, :],
+                    in0=live["y", p, h][:, rows, :],
+                    scalar=gamma_f32[:, 0:1],
+                    in1=x_part[:, rows, :],
+                    op0=ALU.mult,
+                    op1=ALU.add,
+                )
+                nc.sync.dma_start(out=out_part[:, rows, :], in_=result[:, rows, :])
 
         def tile_step(step, i):
             if 0 <= i < N_TILES:
@@ -318,8 +325,7 @@ def tile_selfattention_pb_kernel(tc, q, k, v, Wo, gamma, x, out):
             pair_step(flip_e, c - 4)
             pair_step(project, c - 11, 3)
             if c == 5:
-                quantise_v(0)
-                quantise_v(1)
+                quantise_v()
             pair_step(flip_o, c - 9)
             pair_step(project, c - 11, 2)
             pair_step(finish, c - 12, 3)
@@ -339,8 +345,7 @@ def tile_selfattention_pb_kernel(tc, q, k, v, Wo, gamma, x, out):
             if c in (1, 5):
                 keep_warm()
             if c == 10:
-                for b in range(WO_PAIRS):
-                    quantise_wo(b)
+                quantise_wo()
             if c > 0:
                 tile_step(scores, c)
             pair_step(regroup_o, c - 9)

from contextlib import ExitStack

import concourse.mybir as mybir
from concourse.masks import make_identity

F32 = mybir.dt.float32
BF16 = mybir.dt.bfloat16
U32 = mybir.dt.uint32
U8 = mybir.dt.uint8
FP8X4 = mybir.dt.float8_e4m3fn_x4
ACT = mybir.ActivationFunctionType
ALU = mybir.AluOpType

P = 128
N_POS = 2048
D_QK = 128
K_MX = 512
C_OUT = 1024
HALVES = 2
PACK = 4

N_TILES = N_POS // P
C_TILES = C_OUT // P
V_TILES = K_MX // P
GROUP = 4
N_GROUPS = N_TILES // GROUP
N_HALVES = 2
N_HALF = N_POS // N_HALVES
PAIR = 2
V_PAIRS = V_TILES // PAIR
WO_PAIRS = C_TILES // PAIR
N_PAIRS = N_TILES // PAIR
Y_BANKS = 4
C_PER_BANK = C_TILES // Y_BANKS
W = PAIR * P

Q_RUNS = ((0, 1), (1, 3), (4, 4), (8, 4), (12, 4))
HEAD_WARM = 3

SPARE_TILE = 5
SPARE_PAIR = 3

FLOPS = 2 * N_POS * (D_QK * K_MX + K_MX * K_MX + C_OUT * K_MX)


def tile_selfattention_pb_kernel(tc, q, k, v, Wo, gamma, x, out):
    nc = tc.nc

    q_view = q.rearrange("b (a p) d -> p (b a) d", p=P)
    k_view = k.rearrange("b d m -> d (b m)")
    v_view = v.rearrange("b (t p a) m -> p (b t) a m", p=P, a=PAIR)
    wo_view = Wo.rearrange("(t p a) c -> p t a c", p=P, a=PAIR)
    x_view = x.rearrange("b (t p) h w -> p (b t) (h w)", p=P)
    out_view = out.rearrange("b (t p) h w -> p (b t) (h w)", p=P)

    with ExitStack() as ctx:
        keep = ctx.enter_context(tc.tile_pool(name="keep", bufs=1))
        work = ctx.enter_context(tc.tile_pool(name="work", bufs=N_TILES))
        psum = ctx.enter_context(tc.psum_pool(name="psum", bufs=1))

        ident_bf16 = keep.tile([P, P], BF16, name="ident_bf16")
        ident_f32 = keep.tile([P, P], F32, name="ident_f32")
        q_rows = keep.tile([P, N_TILES, D_QK], BF16, name="q_rows")
        q_flipped = keep.tile([P, N_POS], BF16, name="q_flipped")
        k_sb = keep.tile([P, K_MX], BF16, name="k_sb")
        v_rows = keep.tile([P, V_PAIRS, PAIR, K_MX], BF16, name="v_rows")
        wo_rows = keep.tile([P, WO_PAIRS, PAIR, K_MX], BF16, name="wo_rows")
        x_sb = keep.tile([P, N_HALVES, C_TILES, N_HALF], BF16, name="x_sb")
        gamma_bf16 = keep.tile([P, 1], BF16, name="gamma_bf16")
        gamma_f32 = keep.tile([P, 1], F32, name="gamma_f32")
        v_codes = keep.tile([P, K_MX], U32, name="v_codes", align_bytes=64)
        v_scales = keep.tile([P, K_MX], U8, name="v_scales", align_bytes=64)
        wo_codes = keep.tile([P, C_OUT], U32, name="wo_codes", align_bytes=64)
        wo_scales = keep.tile([P, C_OUT], U8, name="wo_scales", align_bytes=64)
        v_grouped = keep.tile([P, V_TILES * P * PACK], BF16, name="v_grouped", align_bytes=64)
        wo_grouped = keep.tile([P, C_TILES * P * PACK], BF16, name="wo_grouped", align_bytes=64)
        neg_max = keep.tile([P, N_TILES], F32, name="neg_max")
        row_sum = keep.tile([P, N_TILES], F32, name="row_sum")
        inv_sum = keep.tile([P, N_TILES], F32, name="inv_sum")

        nc.scalar.dma_start(out=gamma_bf16[:], in_=gamma.partition_broadcast(P))
        warm_in = keep.tile([P, 1], F32, name="warm_in")
        warm_out = keep.tile([P, 1], F32, name="warm_out")
        nc.vector.memset(warm_in[:], 0.0)
        nc.scalar.activation(out=warm_out[:], in_=warm_in[:], func=ACT.Exp)
        zeros = keep.tile([P, K_MX], BF16, name="zeros")
        nc.vector.memset(zeros[:], 0.0)
        make_identity(nc, ident_bf16[:])
        make_identity(nc, ident_f32[:])

        def load_q(run):
            first, count = Q_RUNS[run]
            tiles = slice(first, first + count)
            nc.sync.dma_start(out=q_rows[:, tiles, :], in_=q_view[:, tiles, :])

        def load_pair(rows, view, b):
            nc.sync.dma_start(out=rows[:, b, :, :], in_=view[:, b, :, :])

        load_q(0)
        nc.sync.dma_start(out=k_sb[:], in_=k_view)
        load_q(1)
        for b in range(V_PAIRS):
            load_pair(v_rows, v_view, b)
        load_q(2)
        for b in range(WO_PAIRS):
            load_pair(wo_rows, wo_view, b)
        load_q(3)
        load_q(4)
        for g in range(N_HALVES):
            for h in range(N_HALVES):
                c_tiles = slice(h * C_TILES // N_HALVES, (h + 1) * C_TILES // N_HALVES)
                nc.sync.dma_start(
                    out=x_sb[:, g, c_tiles, :], in_=x_view[:, c_tiles, g * N_HALF : (g + 1) * N_HALF]
                )
        nc.gpsimd.tensor_copy(out=gamma_f32[:], in_=gamma_bf16[:])

        ctx.enter_context(tc.manual_schedule())

        def keep_warm():
            idle_bank = psum.tile([P, K_MX], F32, name="idle_bank", tag="attn", bufs=1)
            nc.tensor.matmul(out=idle_bank[:], lhsT=zeros[:, 0:P], rhs=zeros[:], start=True, stop=True)

        def flip(row_tiles, tag, bufs):
            bank = psum.tile([P, len(row_tiles), HALVES, P], F32, name="flip_bank", tag=tag, bufs=bufs)
            for a, rows in enumerate(row_tiles):
                words = rows.bitcast(F32)
                for u in range(HALVES):
                    nc.tensor.transpose(
                        out=bank[:, a, u, :], in_=words[:, u * P : (u + 1) * P], identity=ident_f32[:]
                    )
            return bank

        def regroup(copy, bank, grouped, order="p a r u"):
            copy(
                out=grouped.bitcast(F32).rearrange("p (" + order[2:] + ") -> " + order, a=PAIR, u=HALVES),
                in_=bank[:].rearrange("p a u r -> " + order),
            )

        def quantise(grouped, codes, scales):
            nc.vector.quantize_mx(out=codes.bitcast(FP8X4), scales=scales, in_=grouped)

        live = {}

        def flip_v(b):
            live["v_bank", b] = flip([v_rows[:, b, a, :] for a in range(PAIR)], "proj", 3)

        def regroup_v(b):
            part = slice(b * W * PACK, (b + 1) * W * PACK)
            regroup(nc.vector.tensor_copy, live["v_bank", b], v_grouped[:, part], "p r a u")

        def quantise_v():
            quantise(v_grouped[:], v_codes[:], v_scales[:])

        def flip_wo(b):
            live["wo_bank", b] = flip([wo_rows[:, b, a, :] for a in range(PAIR)], "proj", 3)

        def regroup_wo(b):
            copy = nc.scalar.copy if b == 0 else nc.vector.tensor_copy
            part = slice(b * W * PACK, (b + 1) * W * PACK)
            regroup(copy, live["wo_bank", b], wo_grouped[:, part], "p r a u")

        def quantise_wo():
            quantise(wo_grouped[:], wo_codes[:], wo_scales[:])

        def flip_q(run):
            first, count = Q_RUNS[run]
            bank = psum.tile([P, count, P], BF16, name="q_bank", tag="proj", bufs=3)
            for a in range(count):
                nc.tensor.transpose(
                    out=bank[:, a, :], in_=q_rows[:, first + a, :], identity=ident_bf16[:]
                )
            live["q_bank", run] = bank

        def copy_q(run):
            first, count = Q_RUNS[run]
            nc.scalar.copy(
                out=q_flipped[:, first * P : (first + count) * P],
                in_=live["q_bank", run][:].rearrange("p a r -> p (a r)"),
            )

        def scores(i):
            tag = "proj" if i == SPARE_TILE else "scores"
            s_bank = psum.tile([P, K_MX], F32, name="s_bank", tag=tag, bufs=3)
            nc.tensor.matmul(
                out=s_bank[:], lhsT=q_flipped[:, i * P : (i + 1) * P], rhs=k_sb[:], start=True, stop=True
            )
            live["s", i] = s_bank

        def row_maximum(i):
            nc.vector.tensor_reduce(
                out=neg_max[:, i : i + 1],
                in_=live["s", i][:],
                axis=mybir.AxisListType.X,
                op=ALU.max,
                negate=True,
            )

        def exponentials(i):
            e_rows = work.tile([P, K_MX], BF16, name="e_rows")
            nc.scalar.activation(
                out=e_rows[:],
                in_=live["s", i][:],
                func=ACT.Exp,
                bias=neg_max[:, i : i + 1],
                scale=1.0,
                accum_out=row_sum[:, i : i + 1],
            )
            live["e_rows", i] = e_rows

        def flip_e(p):
            live["e_bank", p] = flip([live["e_rows", PAIR * p + a][:] for a in range(PAIR)], "flip", 1)

        def regroup_e(p):
            grouped = work.tile([P, W * PACK], BF16, name="e_grouped", align_bytes=64, bufs=N_PAIRS)
            regroup(nc.scalar.copy, live["e_bank", p], grouped[:])
            live["e_grouped", p] = grouped

        def quantise_e(p):
            e_codes = work.tile([P, W], U32, name="e_codes", align_bytes=64, bufs=N_PAIRS)
            e_scales = work.tile([P, W], U8, name="e_scales", align_bytes=64, bufs=N_PAIRS)
            quantise(live["e_grouped", p][:], e_codes[:], e_scales[:])
            live["e_codes", p] = e_codes
            live["e_scales", p] = e_scales
            tiles = slice(PAIR * p, PAIR * (p + 1))
            nc.vector.reciprocal(out=inv_sum[:, tiles], in_=row_sum[:, tiles])

        def attend(i):
            attn_bank = psum.tile([P, K_MX], F32, name="attn_bank", tag="attn", bufs=1)
            p, a = divmod(i, PAIR)
            cols = slice(a * P, (a + 1) * P)
            nc.tensor.matmul_mx(
                out=attn_bank[:],
                lhsT=live["e_codes", p][:, cols].bitcast(FP8X4),
                lhsT_scale=live["e_scales", p][:, cols],
                rhs=v_codes[:].bitcast(FP8X4),
                rhs_scale=v_scales[:],
                start=True,
                stop=True,
            )
            live["attn", i] = attn_bank

        def divide(i):
            o_rows = work.tile([P, K_MX], BF16, name="o_rows")
            nc.scalar.activation(
                out=o_rows[:], in_=live["attn", i][:], func=ACT.Copy, scale=inv_sum[:, i : i + 1]
            )
            live["o_rows", i] = o_rows

        def flip_o(p):
            live["o_bank", p] = flip([live["o_rows", PAIR * p + a][:] for a in range(PAIR)], "flip", 1)

        def regroup_o(p):
            grouped = work.tile([P, W * PACK], BF16, name="o_grouped", align_bytes=64, bufs=N_PAIRS)
            regroup(nc.scalar.copy, live["o_bank", p], grouped[:])
            live["o_grouped", p] = grouped

        def quantise_o(p):
            o_codes = work.tile([P, W], U32, name="o_codes", align_bytes=64, bufs=N_PAIRS)
            o_scales = work.tile([P, W], U8, name="o_scales", align_bytes=64, bufs=N_PAIRS)
            quantise(live["o_grouped", p][:], o_codes[:], o_scales[:])
            live["o_codes", p] = o_codes
            live["o_scales", p] = o_scales

        def project(p, h):
            tag = "scores" if h == 2 and p >= SPARE_PAIR else "proj"
            y_bank = psum.tile([P, C_PER_BANK, W], F32, name="y_bank", tag=tag, bufs=3)
            for j in range(C_PER_BANK):
                cols = slice((h * C_PER_BANK + j) * P, (h * C_PER_BANK + j + 1) * P)
                nc.tensor.matmul_mx(
                    out=y_bank[:, j, :],
                    lhsT=wo_codes[:, cols].bitcast(FP8X4),
                    lhsT_scale=wo_scales[:, cols],
                    rhs=live["o_codes", p][:].bitcast(FP8X4),
                    rhs_scale=live["o_scales", p][:],
                    start=True,
                    stop=True,
                )
            live["y", p, h] = y_bank

        def finish(p, h):
            g, a = divmod(p, N_PAIRS // N_HALVES)
            c_tiles = slice(h * C_PER_BANK, (h + 1) * C_PER_BANK)
            result = work.tile([P, C_PER_BANK, W], F32, name="result", bufs=Y_BANKS * N_PAIRS)
            x_part = x_sb[:, g, c_tiles, a * W : (a + 1) * W]
            out_part = out_view[:, c_tiles, p * W : (p + 1) * W]
            pieces = C_PER_BANK if (p, h) == (N_PAIRS - 1, 0) else 1
            step = C_PER_BANK // pieces
            for j in range(0, C_PER_BANK, step):
                rows = slice(j, j + step)
                nc.vector.scalar_tensor_tensor(
                    out=result[:, rows, :],
                    in0=live["y", p, h][:, rows, :],
                    scalar=gamma_f32[:, 0:1],
                    in1=x_part[:, rows, :],
                    op0=ALU.mult,
                    op1=ALU.add,
                )
                nc.sync.dma_start(out=out_part[:, rows, :], in_=result[:, rows, :])

        def tile_step(step, i):
            if 0 <= i < N_TILES:
                step(i)

        def pair_step(step, i, *more):
            if 0 <= i < N_TILES and i % PAIR == PAIR - 1:
                step(i // PAIR, *more)

        for step in range(HEAD_WARM):
            keep_warm()
        flip_q(0)
        copy_q(0)
        scores(0)
        flip_q(1)
        copy_q(1)
        for c in range(N_TILES + 13):
            pair_step(quantise_o, c - 11)
            pair_step(project, c - 12, 1)
            if c in (1, 3):
                flip_v(c // 2)
            pair_step(finish, c - 13, 1)
            if c in (2, 4):
                regroup_v(c // 2 - 1)
            tile_step(exponentials, c - 3)
            tile_step(divide, c - 8)
            pair_step(flip_e, c - 4)
            pair_step(project, c - 11, 3)
            if c == 5:
                quantise_v()
            pair_step(flip_o, c - 9)
            pair_step(project, c - 11, 2)
            pair_step(finish, c - 12, 3)
            if c in (4, 6, 8, 10):
                regroup_wo(c // 2 - 2)
            pair_step(finish, c - 12, 2)
            if c in (3, 5, 7, 9):
                flip_wo(c // 2 - 1)
            if c in (3, 6, 8):
                copy_q((c + 1) // 2)
            pair_step(project, c - 12, 0)
            pair_step(regroup_e, c - 4)
            pair_step(finish, c - 13, 0)
            if c in (2, 5, 7):
                flip_q(c // 2 + 1)
            tile_step(row_maximum, c - 1)
            if c in (1, 5):
                keep_warm()
            if c == 10:
                quantise_wo()
            if c > 0:
                tile_step(scores, c)
            pair_step(regroup_o, c - 9)
            pair_step(quantise_e, c - 5)
            tile_step(attend, c - 7)
